import numpy as np
import ml_dtypes


def mxq(x, axis, fmt="e4m3"):
    dtype, down = {"e4m3": (ml_dtypes.float8_e4m3fn, 7), "e5m2": (ml_dtypes.float8_e5m2, 14)}[fmt]
    v = np.moveaxis(np.asarray(x, np.float32).astype(ml_dtypes.bfloat16).astype(np.float64), axis, -1)
    blocks = v.reshape(v.shape[:-1] + (-1, 32))
    amax = np.abs(blocks).max(-1, keepdims=True)
    byte = np.maximum(np.where(amax > 0, np.frexp(amax)[1] - 1 + 127, 0) - down, 1)
    scale = np.exp2(byte - 127.0)
    codes = (blocks / scale).astype(np.float32).astype(dtype).astype(np.float64)
    return np.moveaxis((codes * scale).reshape(v.shape), -1, axis)


WIDE = False


def mx_kscale(k):
    if not WIDE:
        return np.ones(k)
    levels = np.array([10, -10, 5, -5, 0])
    if k % 512:
        return np.exp2(np.random.permutation(np.resize(levels, k // 32))).repeat(32)
    a = np.empty((k // 512, 16))
    for p in range(k // 512):
        a[p, :8] = np.random.permutation(np.resize(levels, 8))
        for g in range(8):
            far = levels[np.abs(levels - a[p, g]) >= 10]
            a[p, g + 8] = far[np.random.randint(len(far))]
    return np.exp2(a.ravel()).repeat(32)


BF16 = ml_dtypes.bfloat16


def bf(x):
    return np.asarray(x, np.float32).astype(BF16)


def f64(x):
    return np.asarray(x).astype(np.float64)


B, N, D, C, H, NS = 2, 1024, 1024, 1024, 16, 10
HD = C // H
D4 = (0.4829629131445341, 0.8365163037378079, 0.2241438680420134, -0.1294095225512604)


def causal_multiscale(x_c, scale_gain):
    g = np.exp(scale_gain - scale_gain.max(0, keepdims=True))
    gains = g / g.sum(0, keepdims=True)
    gains_exp = np.repeat(gains, HD, axis=1)
    out = np.zeros_like(x_c)
    for j in range(NS):
        d = 2 ** j
        xp = np.pad(x_c, ((0, 0), (0, 0), (3 * d, 0)))
        y = (D4[0] * xp[:, :, 0 * d:0 * d + N]
             + D4[1] * xp[:, :, 1 * d:1 * d + N]
             + D4[2] * xp[:, :, 2 * d:2 * d + N]
             + D4[3] * xp[:, :, 3 * d:3 * d + N])
        out = out + gains_exp[j][None, :, None] * y
    return out


def setup_inputs():
    s = mx_kscale(D)
    return {"x": bf(np.random.standard_normal((B, N, D)) * s),
            "k_w": bf(np.random.standard_normal((C, D)) / np.sqrt(D) / s[None, :]),
            "k_b": bf(np.random.standard_normal(C) * 0.2),
            "v_w": bf(np.random.standard_normal((C, D)) / np.sqrt(D) / s[None, :]),
            "v_b": bf(np.random.standard_normal(C) * 0.2),
            "scale_gain": bf(np.random.standard_normal((NS, H)) * 0.5)}


def core(x, k_w, k_b, v_w, v_b, scale_gain):
    xq = mxq(f64(x), 2, "e4m3")
    k = ((xq @ mxq(f64(k_w), 1, "e4m3").T) + f64(k_b)).reshape(B, N, H, HD)
    v = ((xq @ mxq(f64(v_w), 1, "e4m3").T) + f64(v_b)).reshape(B, N, H, HD)
    k_mag = np.sqrt((k * k).sum(-1, keepdims=True))
    field = v * k_mag
    x_c = field.transpose(0, 2, 3, 1).reshape(B, C, N)
    return causal_multiscale(x_c, f64(scale_gain))


def e4m3fn_bytes(y):
    return np.clip(np.asarray(y, np.float64), -448.0, 448.0).astype(np.float32).astype(ml_dtypes.float8_e4m3fn).view(np.uint8)


Y_SCALE = 60.0


def reference(x, k_w, k_b, v_w, v_b, scale_gain):
    out = core(x, k_w, k_b, v_w, v_b, scale_gain)
    return out, e4m3fn_bytes(out * Y_SCALE)

@@ -1,0 +1,160 @@
+from contextlib import ExitStack
+
+import concourse.mybir as mybir
+from concourse.masks import make_identity
+
+B, N, D, C, H, NS = 2, 1024, 1024, 1024, 16, 10
+T0, T1, T2, T3 = 0.4829629131445341, 0.8365163037378079, 0.2241438680420134, -0.1294095225512604
+Y_SCALE = 60.0
+FLOPS = 2 * 2 * B * N * D * C
+
+F32 = mybir.dt.float32
+BF16 = mybir.dt.bfloat16
+U32 = mybir.dt.uint32
+U8 = mybir.dt.uint8
+FP8X4 = mybir.dt.float8_e4m3fn_x4
+FP8 = mybir.dt.float8_e4m3fn
+AF = mybir.ActivationFunctionType
+ALU = mybir.AluOpType
+AX = mybir.AxisListType
+
+P = 128
+NG = 2
+CT = C // P
+QW = 512
+
+
+def tile_causalwaveletfieldattentionbyte_pa_kernel(tc, x, k_w, k_b, v_w, v_b, scale_gain, out_0, out_1):
+    nc = tc.nc
+    xf = x.flatten_outer_dims()
+    NT = B * N
+
+    with ExitStack() as ctx:
+        const = ctx.enter_context(tc.tile_pool(name="const", bufs=1))
+        keep = ctx.enter_context(tc.tile_pool(name="keep", bufs=1))
+        ld = ctx.enter_context(tc.tile_pool(name="ld", bufs=6))
+        work = ctx.enter_context(tc.tile_pool(name="work", bufs=3))
+        pst = ctx.enter_context(tc.psum_pool(name="pst", bufs=2))
+        psm = ctx.enter_context(tc.psum_pool(name="psm", bufs=2))
+
+        ident = const.tile([P, P], F32)
+        make_identity(nc, ident[:])
+        ident_bf = const.tile([P, P], BF16)
+        make_identity(nc, ident_bf[:])
+        ones_blk = const.tile([P, P], F32)
+        nc.vector.memset(ones_blk[:], 0.0)
+        nc.vector.memset(ones_blk[0:64, 0:64], 1.0)
+        nc.vector.memset(ones_blk[64:128, 64:128], 1.0)
+
+        bias_in = const.tile([P, P], BF16)
+        nc.vector.memset(bias_in[:], 0.0)
+        nc.sync.dma_start(out=bias_in[0:CT, :], in_=k_b.rearrange("(c p) -> c p", p=P))
+        nc.sync.dma_start(out=bias_in[CT:2 * CT, :], in_=v_b.rearrange("(c p) -> c p", p=P))
+        sg_bf = const.tile([P, NS * H], BF16)
+        nc.sync.dma_start(out=sg_bf[:], in_=scale_gain.rearrange("j h -> (j h)").partition_broadcast(P))
+
+        bps = pst.tile([P, P], BF16, tag="tp")
+        nc.tensor.transpose(bps[:], bias_in[:], ident_bf[:])
+        bias = const.tile([P, 2 * CT], F32)
+        nc.vector.tensor_copy(out=bias[:], in_=bps[:, 0:2 * CT])
+
+        sg = const.tile([P, H, NS], F32)
+        nc.vector.tensor_copy(out=sg[:], in_=sg_bf[:].rearrange("p (j h) -> p h j", h=H))
+        mx = const.tile([P, H], F32)
+        nc.vector.tensor_reduce(out=mx[:], in_=sg[:], axis=AX.X, op=ALU.max)
+        nc.vector.tensor_tensor(out=sg[:], in0=sg[:], in1=mx[:].unsqueeze(2).to_broadcast([P, H, NS]), op=ALU.subtract)
+        eg = const.tile([P, H, NS], F32)
+        nc.scalar.activation(out=eg[:], in_=sg[:], func=AF.Exp)
+        sm = const.tile([P, H], F32)
+        nc.vector.tensor_reduce(out=sm[:], in_=eg[:], axis=AX.X, op=ALU.add)
+        rs = const.tile([P, H], F32)
+        nc.vector.reciprocal(out=rs[:], in_=sm[:])
+        nc.vector.tensor_tensor(out=eg[:], in0=eg[:], in1=rs[:].unsqueeze(2).to_broadcast([P, H, NS]), op=ALU.mult)
+        gsel = const.tile([P, CT, NS], F32)
+        for s in range(2):
+            rows = slice(64 * s, 64 * s + 64)
+            nc.vector.tensor_copy(out=gsel[rows], in_=eg[rows].rearrange("p (c s) j -> p s c j", s=2)[:, s])
+        ca = const.tile([P, CT, NS], F32)
+        nc.vector.tensor_scalar(out=ca[:], in0=gsel[:], scalar1=T2, scalar2=None, op0=ALU.mult)
+        nc.vector.scalar_tensor_tensor(out=ca[:, :, 1:NS], in0=gsel[:, :, 0:NS - 1], scalar=T1, in1=ca[:, :, 1:NS],
+                                       op0=ALU.mult, op1=ALU.add)
+        cb = const.tile([P, CT, NS], F32)
+        nc.vector.tensor_scalar(out=cb[:], in0=gsel[:], scalar1=T0, scalar2=None, op0=ALU.mult)
+
+        xg = keep.tile([P, NG, NT * 4], BF16, align_bytes=64)
+        xc = keep.tile([P, NG, NT], U32, align_bytes=64)
+        xs = keep.tile([P, NG, NT], U8, align_bytes=64)
+        kg = keep.tile([P, NG, C * 4], BF16, align_bytes=64)
+        kc = keep.tile([P, NG, C], U32, align_bytes=64)
+        ks = keep.tile([P, NG, C], U8, align_bytes=64)
+        vg = keep.tile([P, NG, C * 4], BF16, align_bytes=64)
+        vc = keep.tile([P, NG, C], U32, align_bytes=64)
+        vs = keep.tile([P, NG, C], U8, align_bytes=64)
+
+        def turn(src, grouped, rt):
+            raw = ld.tile([P, D], BF16)
+            nc.sync.dma_start(out=raw[:], in_=src[rt * P:(rt + 1) * P, :])
+            words = raw[:].bitcast(F32)
+            tp = pst.tile([P, NG, 2, P], F32, tag="tp")
+            for g in range(NG):
+                for u in range(2):
+                    nc.tensor.transpose(tp[:, g, u, :], words[:, 256 * g + u:256 * (g + 1):2], ident[:])
+            dst = grouped[:].bitcast(F32)[:, :, 2 * P * rt:2 * P * (rt + 1)].rearrange("p g (r u) -> p g r u", u=2)
+            nc.scalar.copy(out=dst, in_=tp[:].rearrange("p g u r -> p g r u"))
+
+        def quant(grouped, codes, scales, q):
+            for g in range(NG):
+                cols = slice(q * QW, (q + 1) * QW)
+                nc.vector.quantize_mx(out=codes[:, g, cols].bitcast(FP8X4), scales=scales[:, g, cols],
+                                      in_=grouped[:, g, 4 * q * QW:4 * (q + 1) * QW])
+
+        def prepare(src, grouped, codes, scales, q):
+            for rt in range(4 * q, 4 * q + 4):
+                turn(src, grouped, rt)
+            quant(grouped, codes, scales, q)
+
+        prepare(k_w, kg, kc, ks, 0)
+        prepare(v_w, vg, vc, vs, 0)
+        prepare(xf, xg, xc, xs, 0)
+        prepare(xf, xg, xc, xs, 1)
+        prepare(k_w, kg, kc, ks, 1)
+        prepare(v_w, vg, vc, vs, 1)
+        prepare(xf, xg, xc, xs, 2)
+        prepare(xf, xg, xc, xs, 3)
+
+        lags = [(2 ** j, ca, j) for j in range(NS)] + [(3 * 2 ** j, cb, j) for j in range(NS - 1)]
+
+        for b in range(B):
+            for ct in range(CT):
+                ch = slice(ct * P, (ct + 1) * P)
+                f = work.tile([P, N], F32)
+                for hf in range(2):
+                    tok = slice(b * N + hf * 512, b * N + (hf + 1) * 512)
+                    kps = psm.tile([P, 512], F32)
+                    vps = psm.tile([P, 512], F32)
+                    for g in range(NG):
+                        nc.tensor.matmul_mx(out=kps[:], lhsT=kc[:, g, ch].bitcast(FP8X4), lhsT_scale=ks[:, g, ch],
+                                            rhs=xc[:, g, tok].bitcast(FP8X4), rhs_scale=xs[:, g, tok],
+                                            start=(g == 0), stop=(g == NG - 1))
+                    for g in range(NG):
+                        nc.tensor.matmul_mx(out=vps[:], lhsT=vc[:, g, ch].bitcast(FP8X4), lhsT_scale=vs[:, g, ch],
+                                            rhs=xc[:, g, tok].bitcast(FP8X4), rhs_scale=xs[:, g, tok],
+                                            start=(g == 0), stop=(g == NG - 1))
+                    k2 = work.tile([P, 512], F32)
+                    nc.scalar.activation(out=k2[:], in_=kps[:], func=AF.Square, bias=bias[:, ct:ct + 1], scale=1.0)
+                    m2 = psm.tile([P, 512], F32)
+                    nc.tensor.matmul(out=m2[:], lhsT=ones_blk[:], rhs=k2[:], start=True, stop=True)
+                    mm = work.tile([P, 512], F32)
+                    nc.scalar.activation(out=mm[:], in_=m2[:], func=AF.Sqrt)
+                    nc.vector.scalar_tensor_tensor(out=f[:, hf * 512:(hf + 1) * 512], in0=vps[:],
+                                                   scalar=bias[:, CT + ct:CT + ct + 1], in1=mm[:],
+                                                   op0=ALU.add, op1=ALU.mult)
+                acc = work.tile([P, N], F32)
+                nc.scalar.activation(out=acc[:], in_=f[:], func=AF.Copy, scale=T3)
+                for lag, co, j in lags:
+                    nc.vector.scalar_tensor_tensor(out=acc[:, lag:N], in0=f[:, 0:N - lag], scalar=co[:, ct, j:j + 1],
+                                                   in1=acc[:, lag:N], op0=ALU.mult, op1=ALU.add)
+                nc.sync.dma_start(out=out_0[b, ch, :], in_=acc[:])
+                o8 = work.tile([P, N], FP8)
+                nc.scalar.activation(out=o8[:], in_=acc[:], func=AF.Copy, scale=Y_SCALE, saturate=False)
+                nc.sync.dma_start(out=out_1[b, ch, :], in_=o8[:].bitcast(U8))

@@ -17,46 +17,91 @@ FP8 = mybir.dt.float8_e4m3fn
 AF = mybir.ActivationFunctionType
 ALU = mybir.AluOpType
 AX = mybir.AxisListType
+ET = mybir.EngineType
 
 P = 128
 NG = 2
 CT = C // P
 QW = 512
+R = 8
+TT = B * R
+PAD = 16
 
 
 def tile_causalwaveletfieldattentionbyte_pa_kernel(tc, x, k_w, k_b, v_w, v_b, scale_gain, out_0, out_1):
     nc = tc.nc
-    xf = x.flatten_outer_dims()
     NT = B * N
 
     with ExitStack() as ctx:
         const = ctx.enter_context(tc.tile_pool(name="const", bufs=1))
         keep = ctx.enter_context(tc.tile_pool(name="keep", bufs=1))
-        ld = ctx.enter_context(tc.tile_pool(name="ld", bufs=6))
+        ld = ctx.enter_context(tc.tile_pool(name="ld", bufs=1))
+        stg = ctx.enter_context(tc.tile_pool(name="stg", bufs=3))
         work = ctx.enter_context(tc.tile_pool(name="work", bufs=3))
-        pst = ctx.enter_context(tc.psum_pool(name="pst", bufs=2))
-        psm = ctx.enter_context(tc.psum_pool(name="psm", bufs=2))
+        two = ctx.enter_context(tc.tile_pool(name="two", bufs=2))
+        four = ctx.enter_context(tc.tile_pool(name="four", bufs=4))
+        pss = ctx.enter_context(tc.psum_pool(name="pss", bufs=4))
+        psv = ctx.enter_context(tc.psum_pool(name="psv", bufs=4))
 
-        ident = const.tile([P, P], F32)
-        make_identity(nc, ident[:])
-        ident_bf = const.tile([P, P], BF16)
-        make_identity(nc, ident_bf[:])
-        ones_blk = const.tile([P, P], F32)
-        nc.vector.memset(ones_blk[:], 0.0)
-        nc.vector.memset(ones_blk[0:64, 0:64], 1.0)
-        nc.vector.memset(ones_blk[64:128, 64:128], 1.0)
+        kview = k_w.rearrange("(t p) d -> p t d", p=P)
+        vview = v_w.rearrange("(t p) d -> p t d", p=P)
+        xviews = [x[b].rearrange("(q r) d -> q r d", r=R) for b in range(B)]
+        groups = [(kview, 0, "k"), (xviews[0], 0, "x0"), (xviews[0], 1, "x0"), (vview, 0, "v"),
+                  (kview, 1, "k"), (vview, 1, "v"), (xviews[1], 0, "x1"), (xviews[1], 1, "x1")]
+        raws = []
+        for gi in range(len(groups)):
+            view, q, kind = groups[gi]
+            pair = []
+            for half in range(2):
+                raw = ld.tile([P, 2, D], BF16, name="raw%d_%d" % (gi, half))
+                nc.sync.dma_start(out=raw[:], in_=view[:, 4 * q + 2 * half:4 * q + 2 * half + 2, :])
+                pair.append(raw)
+            raws.append(pair)
 
         bias_in = const.tile([P, P], BF16)
         nc.vector.memset(bias_in[:], 0.0)
-        nc.sync.dma_start(out=bias_in[0:CT, :], in_=k_b.rearrange("(c p) -> c p", p=P))
-        nc.sync.dma_start(out=bias_in[CT:2 * CT, :], in_=v_b.rearrange("(c p) -> c p", p=P))
+        nc.scalar.dma_start(out=bias_in[0:CT, :], in_=k_b.rearrange("(c p) -> c p", p=P))
         sg_bf = const.tile([P, NS * H], BF16)
-        nc.sync.dma_start(out=sg_bf[:], in_=scale_gain.rearrange("j h -> (j h)").partition_broadcast(P))
+        nc.scalar.dma_start(out=sg_bf[:], in_=scale_gain.rearrange("j h -> (j h)").partition_broadcast(P))
+        vbc = const.tile([P, C], BF16)
+        nc.scalar.dma_start(out=vbc[:], in_=v_b.partition_broadcast(P))
 
-        bps = pst.tile([P, P], BF16, tag="tp")
+        ipad = const.tile([P, 2 * P], F32)
+        nc.gpsimd.memset(ipad[:], 0.0)
+        make_identity(nc, ipad[:, P:2 * P])
+        ident = ipad[:, P:2 * P]
+
+        def shifted(dq):
+            return ipad[:, P - dq:2 * P - dq]
+
+        ident_bf = const.tile([P, P], BF16)
+        make_identity(nc, ident_bf[:])
+        sel2 = const.tile([P, 2], F32)
+        nc.vector.memset(sel2[:], 0.0)
+        nc.vector.memset(sel2[0:64, 0:1], 1.0)
+        nc.vector.memset(sel2[64:128, 1:2], 1.0)
+        fsb = []
+        for i in range(3):
+            t = const.tile([P, PAD + N], F32, name="fsb%d" % i)
+            nc.vector.memset(t[:, 0:PAD], 0.0)
+            fsb.append(t)
+
+        yc = const.tile([P, R, P], F32)
+        nc.vector.tensor_scalar(out=yc[:, 0, :], in0=shifted(1), scalar1=T1, scalar2=None, op0=ALU.mult)
+        for i in range(1, 8):
+            dq = 2 ** (i - 1)
+            nc.vector.tensor_scalar(out=yc[:, i, :], in0=shifted(dq), scalar1=T2, scalar2=None, op0=ALU.mult)
+            for mul, tap in ((2, T1), (3, T0)):
+                if mul * dq < P:
+                    nc.vector.scalar_tensor_tensor(out=yc[:, i, :], in0=shifted(mul * dq), scalar=tap, in1=yc[:, i, :],
+                                                   op0=ALU.mult, op1=ALU.add)
+        t3i = const.tile([P, P], F32)
+        nc.vector.tensor_scalar(out=t3i[:], in0=ident, scalar1=T3, scalar2=None, op0=ALU.mult)
+
+        bps = psv.tile([P, P], BF16, tag="v")
         nc.tensor.transpose(bps[:], bias_in[:], ident_bf[:])
-        bias = const.tile([P, 2 * CT], F32)
-        nc.vector.tensor_copy(out=bias[:], in_=bps[:, 0:2 * CT])
+        kbias = const.tile([P, CT], F32)
+        nc.vector.tensor_copy(out=kbias[:], in_=bps[:, 0:CT])
 
         sg = const.tile([P, H, NS], F32)
         nc.vector.tensor_copy(out=sg[:], in_=sg_bf[:].rearrange("p (j h) -> p h j", h=H))
@@ -81,80 +126,240 @@ def tile_causalwaveletfieldattentionbyte_pa_kernel(tc, x, k_w, k_b, v_w, v_b, sc
         cb = const.tile([P, CT, NS], F32)
         nc.vector.tensor_scalar(out=cb[:], in0=gsel[:], scalar1=T0, scalar2=None, op0=ALU.mult)
 
-        xg = keep.tile([P, NG, NT * 4], BF16, align_bytes=64)
+        th = const.tile([P, H, P], F32)
+
+        def build_t(h):
+            nc.vector.scalar_tensor_tensor(out=th[:, h, :], in0=yc[:, 0, :], scalar=eg[:, h, 2:3], in1=t3i[:],
+                                           op0=ALU.mult, op1=ALU.add)
+            for i in range(1, 8):
+                dq = 2 ** (i - 1)
+                nc.vector.scalar_tensor_tensor(out=th[:, h, dq:P], in0=yc[:, i, dq:P], scalar=eg[:, h, i + 2:i + 3],
+                                               in1=th[:, h, dq:P], op0=ALU.mult, op1=ALU.add)
+
         xc = keep.tile([P, NG, NT], U32, align_bytes=64)
         xs = keep.tile([P, NG, NT], U8, align_bytes=64)
-        kg = keep.tile([P, NG, C * 4], BF16, align_bytes=64)
         kc = keep.tile([P, NG, C], U32, align_bytes=64)
         ks = keep.tile([P, NG, C], U8, align_bytes=64)
-        vg = keep.tile([P, NG, C * 4], BF16, align_bytes=64)
         vc = keep.tile([P, NG, C], U32, align_bytes=64)
         vs = keep.tile([P, NG, C], U8, align_bytes=64)
+        dest = {"k": (kc, ks, 0), "v": (vc, vs, 0), "x0": (xc, xs, 0), "x1": (xc, xs, N)}
 
-        def turn(src, grouped, rt):
-            raw = ld.tile([P, D], BF16)
-            nc.sync.dma_start(out=raw[:], in_=src[rt * P:(rt + 1) * P, :])
-            words = raw[:].bitcast(F32)
-            tp = pst.tile([P, NG, 2, P], F32, tag="tp")
-            for g in range(NG):
-                for u in range(2):
-                    nc.tensor.transpose(tp[:, g, u, :], words[:, 256 * g + u:256 * (g + 1):2], ident[:])
-            dst = grouped[:].bitcast(F32)[:, :, 2 * P * rt:2 * P * (rt + 1)].rearrange("p g (r u) -> p g r u", u=2)
-            nc.scalar.copy(out=dst, in_=tp[:].rearrange("p g u r -> p g r u"))
+        grouped_of = {}
 
-        def quant(grouped, codes, scales, q):
+        def prepare_a(gi):
+            grouped = stg.tile([P, NG, 4 * QW], BF16, align_bytes=64)
+            grouped_of[gi] = grouped
+            gw = grouped[:].bitcast(F32)
+            for i in range(4):
+                words = raws[gi][i // 2][:, i % 2, :].bitcast(F32)
+                if gi < 6 and i % 2:
+                    tp = psv.tile([P, NG, 2, P], F32, tag="v")
+                else:
+                    tp = pss.tile([P, NG, 2, P], F32, tag="s")
+                for g in range(NG):
+                    for u in range(2):
+                        nc.tensor.transpose(tp[:, g, u, :], words[:, 256 * g + u:256 * (g + 1):2], ident)
+                dst = gw[:, :, 2 * P * i:2 * P * (i + 1)].rearrange("p g (r u) -> p g r u", u=2)
+                nc.scalar.copy(out=dst, in_=tp[:].rearrange("p g u r -> p g r u"))
+
+        def prepare_b(gi):
+            view, q, kind = groups[gi]
+            codes, scales, base = dest[kind]
+            cols = slice(base + q * QW, base + (q + 1) * QW)
             for g in range(NG):
-                cols = slice(q * QW, (q + 1) * QW)
                 nc.vector.quantize_mx(out=codes[:, g, cols].bitcast(FP8X4), scales=scales[:, g, cols],
-                                      in_=grouped[:, g, 4 * q * QW:4 * (q + 1) * QW])
+                                      in_=grouped_of[gi][:, g, :])
 
-        def prepare(src, grouped, codes, scales, q):
-            for rt in range(4 * q, 4 * q + 4):
-                turn(src, grouped, rt)
-            quant(grouped, codes, scales, q)
+        def prepare(gi):
+            prepare_a(gi)
+            prepare_b(gi)
 
-        prepare(k_w, kg, kc, ks, 0)
-        prepare(v_w, vg, vc, vs, 0)
-        prepare(xf, xg, xc, xs, 0)
-        prepare(xf, xg, xc, xs, 1)
-        prepare(k_w, kg, kc, ks, 1)
-        prepare(v_w, vg, vc, vs, 1)
-        prepare(xf, xg, xc, xs, 2)
-        prepare(xf, xg, xc, xs, 3)
+        NU = B * CT
+        k2_of, mt_of, ft_of, gt_of, tp_of, acc_of, m2_of, vps_of, m2c_of = {}, {}, {}, {}, {}, {}, {}, {}, {}
 
-        lags = [(2 ** j, ca, j) for j in range(NS)] + [(3 * 2 ** j, cb, j) for j in range(NS - 1)]
+        def k_mx(u, c):
+            if u < 0 or u >= NU:
+                return
+            b, hp = u // CT, u % CT
+            ch = slice(hp * P, (hp + 1) * P)
+            if c == 0:
+                k2 = work.tile([P, N], F32, name="k2")
+                k2_of[u] = k2
+            tok = slice(b * N + c * 512, b * N + (c + 1) * 512)
+            kps = pss.tile([P, 512], F32, tag="s")
+            for g in range(NG):
+                nc.tensor.matmul_mx(out=kps[:], lhsT=kc[:, g, ch].bitcast(FP8X4), lhsT_scale=ks[:, g, ch],
+                                    rhs=xc[:, g, tok].bitcast(FP8X4), rhs_scale=xs[:, g, tok],
+                                    start=(g == 0), stop=(g == NG - 1))
+            nc.scalar.activation(out=k2_of[u][:, c * 512:(c + 1) * 512], in_=kps[:], func=AF.Square,
+                                 bias=kbias[:, hp:hp + 1], scale=1.0)
 
-        for b in range(B):
-            for ct in range(CT):
-                ch = slice(ct * P, (ct + 1) * P)
-                f = work.tile([P, N], F32)
-                for hf in range(2):
-                    tok = slice(b * N + hf * 512, b * N + (hf + 1) * 512)
-                    kps = psm.tile([P, 512], F32)
-                    vps = psm.tile([P, 512], F32)
-                    for g in range(NG):
-                        nc.tensor.matmul_mx(out=kps[:], lhsT=kc[:, g, ch].bitcast(FP8X4), lhsT_scale=ks[:, g, ch],
-                                            rhs=xc[:, g, tok].bitcast(FP8X4), rhs_scale=xs[:, g, tok],
-                                            start=(g == 0), stop=(g == NG - 1))
-                    for g in range(NG):
-                        nc.tensor.matmul_mx(out=vps[:], lhsT=vc[:, g, ch].bitcast(FP8X4), lhsT_scale=vs[:, g, ch],
-                                            rhs=xc[:, g, tok].bitcast(FP8X4), rhs_scale=xs[:, g, tok],
-                                            start=(g == 0), stop=(g == NG - 1))
-                    k2 = work.tile([P, 512], F32)
-                    nc.scalar.activation(out=k2[:], in_=kps[:], func=AF.Square, bias=bias[:, ct:ct + 1], scale=1.0)
-                    m2 = psm.tile([P, 512], F32)
-                    nc.tensor.matmul(out=m2[:], lhsT=ones_blk[:], rhs=k2[:], start=True, stop=True)
-                    mm = work.tile([P, 512], F32)
-                    nc.scalar.activation(out=mm[:], in_=m2[:], func=AF.Sqrt)
-                    nc.vector.scalar_tensor_tensor(out=f[:, hf * 512:(hf + 1) * 512], in0=vps[:],
-                                                   scalar=bias[:, CT + ct:CT + ct + 1], in1=mm[:],
-                                                   op0=ALU.add, op1=ALU.mult)
-                acc = work.tile([P, N], F32)
-                nc.scalar.activation(out=acc[:], in_=f[:], func=AF.Copy, scale=T3)
-                for lag, co, j in lags:
-                    nc.vector.scalar_tensor_tensor(out=acc[:, lag:N], in0=f[:, 0:N - lag], scalar=co[:, ct, j:j + 1],
-                                                   in1=acc[:, lag:N], op0=ALU.mult, op1=ALU.add)
-                nc.sync.dma_start(out=out_0[b, ch, :], in_=acc[:])
-                o8 = work.tile([P, N], FP8)
-                nc.scalar.activation(out=o8[:], in_=acc[:], func=AF.Copy, scale=Y_SCALE, saturate=False)
-                nc.sync.dma_start(out=out_1[b, ch, :], in_=o8[:].bitcast(U8))
+        def sel_pe(u):
+            if u < 0 or u >= NU:
+                return
+            m2 = psv.tile([P, R, 2], F32, tag="v")
+            m2_of[u] = m2
+            for r in range(R):
+                nc.tensor.matmul(out=m2[:, r, :], lhsT=k2_of[u][:, r * P:(r + 1) * P], rhs=sel2[:], start=True, stop=True)
+
+        def sel_v(u):
+            if u < 0 or u >= NU:
+                return
+            m2c = four.tile([P, R, 2], F32, name="m2c")
+            m2c_of[u] = m2c
+            nc.vector.tensor_scalar(out=m2c[:], in0=m2_of[u][:], scalar1=1e-30, scalar2=None, op0=ALU.max)
+
+        def sel_s(u):
+            if u < 0 or u >= NU:
+                return
+            mt = four.tile([P, R, 2], F32, name="mt")
+            nc.scalar.activation(out=mt[:], in_=m2c_of[u][:], func=AF.Sqrt)
+            mt_of[u] = mt
+
+        def v_pe(u, c):
+            if u < 0 or u >= NU:
+                return
+            b, hp = u // CT, u % CT
+            ch = slice(hp * P, (hp + 1) * P)
+            vps = psv.tile([P, 4, P], F32, tag="v")
+            vps_of[(u, c)] = vps
+            for i in range(4):
+                t0 = b * N + (4 * c + i) * P
+                tok = slice(t0, t0 + P)
+                for g in range(NG):
+                    nc.tensor.matmul_mx(out=vps[:, i, :], lhsT=xc[:, g, tok].bitcast(FP8X4), lhsT_scale=xs[:, g, tok],
+                                        rhs=vc[:, g, ch].bitcast(FP8X4), rhs_scale=vs[:, g, ch],
+                                        start=(g == 0), stop=(g == NG - 1))
+
+        def v_vs(u, c):
+            if u < 0 or u >= NU:
+                return
+            hp = u % CT
+            ch = slice(hp * P, (hp + 1) * P)
+            if c == 0:
+                ft = four.tile([P, R, P], F32, name="ft")
+                ft_of[u] = ft
+            vb = work.tile([P, 4, P], F32)
+            nc.vector.tensor_tensor(out=vb[:], in0=vps_of[(u, c)][:], in1=vbc[:, ch].unsqueeze(1).to_broadcast([P, 4, P]),
+                                    op=ALU.add)
+            for i in range(4):
+                r = 4 * c + i
+                for s in range(2):
+                    nc.scalar.activation(out=ft_of[u][:, r, 64 * s:64 * s + 64], in_=vb[:, i, 64 * s:64 * s + 64],
+                                         func=AF.Copy, scale=mt_of[u][:, r, s:s + 1])
+
+        def g_mm(u, s):
+            if u < 0 or u >= NU:
+                return
+            hp = u % CT
+            if s == 0:
+                gt = work.tile([P, R, P], F32, name="gt")
+                gt_of[u] = gt
+            gps = pss.tile([P, R, 64], F32, tag="s")
+            nc.tensor.matmul(out=gps[:], lhsT=th[:, 2 * hp + s, :], rhs=ft_of[u][:, :, 64 * s:64 * s + 64],
+                             start=True, stop=True)
+            nc.scalar.copy(out=gt_of[u][:, :, 64 * s:64 * s + 64], in_=gps[:])
+
+        def c_f(u, half):
+            if u < 0 or u >= NU:
+                return
+            fsv = fsb[u % 3][:, PAD:PAD + N].rearrange("p (q r) -> p q r", r=R)
+            fp = pss.tile([P, 4, P], F32, tag="s")
+            for i in range(4):
+                nc.tensor.transpose(fp[:, i, :], ft_of[u][:, 4 * half + i, :], ident)
+            nc.scalar.copy(out=fsv[:, :, 4 * half:4 * half + 4], in_=fp[:].rearrange("p r q -> p q r"))
+
+        def c_g(u, half):
+            if u < 0 or u >= NU:
+                return
+            tp = psv.tile([P, 4, P], F32, tag="v")
+            for i in range(4):
+                nc.tensor.transpose(tp[:, i, :], gt_of[u][:, 4 * half + i, :], ident)
+            tp_of[(u, half)] = tp
+
+        def v_first(u):
+            hp = u % CT
+            f1v = fsb[u % 3][:, PAD - 1:PAD - 1 + N].rearrange("p (q r) -> p q r", r=R)
+            acc = work.tile([P, N], F32)
+            acc_of[u] = acc
+            accv = acc[:].rearrange("p (q r) -> p q r", r=R)
+            for half in range(2):
+                nc.vector.scalar_tensor_tensor(out=accv[:, :, 4 * half:4 * half + 4], in0=f1v[:, :, 4 * half:4 * half + 4],
+                                               scalar=ca[:, hp, 0:1], in1=tp_of[(u, half)][:].rearrange("p r q -> p q r"),
+                                               op0=ALU.mult, op1=ALU.add)
+
+        short = ((2, ca, 1), (3, cb, 0), (4, ca, 2), (6, cb, 1), (12, cb, 2))
+
+        def v_lag(u, i):
+            lag, co, j = short[i]
+            acc = acc_of[u]
+            nc.vector.scalar_tensor_tensor(out=acc[:], in0=fsb[u % 3][:, PAD - lag:PAD - lag + N],
+                                           scalar=co[:, u % CT, j:j + 1], in1=acc[:], op0=ALU.mult, op1=ALU.add)
+
+        def fin0(u):
+            b, hp = u // CT, u % CT
+            nc.sync.dma_start(out=out_0[b, hp * P:(hp + 1) * P, :], in_=acc_of[u][:])
+
+        def fin1(u):
+            if u < 0:
+                return
+            b, hp = u // CT, u % CT
+            o8 = work.tile([P, N], FP8)
+            nc.scalar.activation(out=o8[:], in_=acc_of[u][:], func=AF.Copy, scale=Y_SCALE, saturate=False)
+            nc.sync.dma_start(out=out_1[b, hp * P:(hp + 1) * P, :], in_=o8[:].bitcast(U8))
+
+
+        def step(t):
+            sel_pe(t + 4)
+            if t >= 0:
+                v_first(t)
+            sel_v(t + 4)
+            v_pe(t + 3, 0)
+            k_mx(t + 5, 0)
+            v_pe(t + 3, 1)
+            k_mx(t + 5, 1)
+            c_f(t + 1, 0)
+            c_g(t + 1, 0)
+            c_f(t + 1, 1)
+            c_g(t + 1, 1)
+            g_mm(t + 2, 0)
+            g_mm(t + 2, 1)
+            sel_s(t + 4)
+            if t >= 0:
+                v_lag(t, 0)
+            v_vs(t + 3, 0)
+            if t >= 0:
+                v_lag(t, 1)
+            v_vs(t + 3, 1)
+            if t >= 0:
+                v_lag(t, 2)
+                v_lag(t, 3)
+                fin1(t - 1)
+            if 0 <= t < 3:
+                prepare_b(t + 5)
+            if t >= 0:
+                v_lag(t, 4)
+                fin0(t)
+            if 0 <= t < 2:
+                prepare_a(t + 6)
+
+        with tc.manual_schedule(engines={ET.PE, ET.Activation, ET.SP, ET.Pool}):
+            prepare(0)
+            prepare(1)
+            prepare(2)
+            for h in range(4):
+                build_t(h)
+            step(-5)
+            prepare(3)
+            step(-4)
+            step(-3)
+            prepare(4)
+            step(-2)
+            prepare_a(5)
+            step(-1)
+            for h in range(4, H):
+                build_t(h)
+        with tc.manual_schedule():
+            for t in range(NU):
+                step(t)
+            fin1(NU - 1)

@@ -76,6 +76,8 @@ def tile_causalwaveletfieldattentionbyte_pa_kernel(tc, x, k_w, k_b, v_w, v_b, sc
 
         ident_bf = const.tile([P, P], BF16)
         make_identity(nc, ident_bf[:])
+        tiny = const.tile([P, 1], F32)
+        nc.vector.memset(tiny[:], 1e-30)
         sel2 = const.tile([P, 2], F32)
         nc.vector.memset(sel2[:], 0.0)
         nc.vector.memset(sel2[0:64, 0:1], 1.0)
@@ -128,13 +130,19 @@ def tile_causalwaveletfieldattentionbyte_pa_kernel(tc, x, k_w, k_b, v_w, v_b, sc
 
         th = const.tile([P, H, P], F32)
 
-        def build_t(h):
-            nc.vector.scalar_tensor_tensor(out=th[:, h, :], in0=yc[:, 0, :], scalar=eg[:, h, 2:3], in1=t3i[:],
-                                           op0=ALU.mult, op1=ALU.add)
-            for i in range(1, 8):
-                dq = 2 ** (i - 1)
-                nc.vector.scalar_tensor_tensor(out=th[:, h, dq:P], in0=yc[:, i, dq:P], scalar=eg[:, h, i + 2:i + 3],
-                                               in1=th[:, h, dq:P], op0=ALU.mult, op1=ALU.add)
+        built = [0]
+
+        def fill(n):
+            for c in range(built[0], min(built[0] + n, 8 * H)):
+                h, i = 4 * (c // 32) + c % 4, (c % 32) // 4
+                if i == 0:
+                    nc.vector.scalar_tensor_tensor(out=th[:, h, :], in0=yc[:, 0, :], scalar=eg[:, h, 2:3], in1=t3i[:],
+                                                   op0=ALU.mult, op1=ALU.add)
+                else:
+                    dq = 2 ** (i - 1)
+                    nc.vector.scalar_tensor_tensor(out=th[:, h, dq:P], in0=yc[:, i, dq:P], scalar=eg[:, h, i + 2:i + 3],
+                                                   in1=th[:, h, dq:P], op0=ALU.mult, op1=ALU.add)
+            built[0] = min(built[0] + n, 8 * H)
 
         xc = keep.tile([P, NG, NT], U32, align_bytes=64)
         xs = keep.tile([P, NG, NT], U8, align_bytes=64)
@@ -202,18 +210,11 @@ def tile_causalwaveletfieldattentionbyte_pa_kernel(tc, x, k_w, k_b, v_w, v_b, sc
             for r in range(R):
                 nc.tensor.matmul(out=m2[:, r, :], lhsT=k2_of[u][:, r * P:(r + 1) * P], rhs=sel2[:], start=True, stop=True)
 
-        def sel_v(u):
-            if u < 0 or u >= NU:
-                return
-            m2c = four.tile([P, R, 2], F32, name="m2c")
-            m2c_of[u] = m2c
-            nc.vector.tensor_scalar(out=m2c[:], in0=m2_of[u][:], scalar1=1e-30, scalar2=None, op0=ALU.max)
-
         def sel_s(u):
             if u < 0 or u >= NU:
                 return
             mt = four.tile([P, R, 2], F32, name="mt")
-            nc.scalar.activation(out=mt[:], in_=m2c_of[u][:], func=AF.Sqrt)
+            nc.scalar.activation(out=mt[:], in_=m2_of[u][:], func=AF.Sqrt, bias=tiny[:, 0:1], scale=1.0)
             mt_of[u] = mt
 
         def v_pe(u, c):
@@ -293,8 +294,10 @@ def tile_causalwaveletfieldattentionbyte_pa_kernel(tc, x, k_w, k_b, v_w, v_b, sc
         def v_lag(u, i):
             lag, co, j = short[i]
             acc = acc_of[u]
-            nc.vector.scalar_tensor_tensor(out=acc[:], in0=fsb[u % 3][:, PAD - lag:PAD - lag + N],
-                                           scalar=co[:, u % CT, j:j + 1], in1=acc[:], op0=ALU.mult, op1=ALU.add)
+            for c0 in (0, N // 2):
+                nc.vector.scalar_tensor_tensor(out=acc[:, c0:c0 + N // 2], in0=fsb[u % 3][:, PAD - lag + c0:PAD - lag + c0 + N // 2],
+                                               scalar=co[:, u % CT, j:j + 1], in1=acc[:, c0:c0 + N // 2],
+                                               op0=ALU.mult, op1=ALU.add)
 
         def fin0(u):
             b, hp = u // CT, u % CT
@@ -313,7 +316,6 @@ def tile_causalwaveletfieldattentionbyte_pa_kernel(tc, x, k_w, k_b, v_w, v_b, sc
             sel_pe(t + 4)
             if t >= 0:
                 v_first(t)
-            sel_v(t + 4)
             v_pe(t + 3, 0)
             k_mx(t + 5, 0)
             v_pe(t + 3, 1)
@@ -325,16 +327,19 @@ def tile_causalwaveletfieldattentionbyte_pa_kernel(tc, x, k_w, k_b, v_w, v_b, sc
             g_mm(t + 2, 0)
             g_mm(t + 2, 1)
             sel_s(t + 4)
-            if t >= 0:
-                v_lag(t, 0)
             v_vs(t + 3, 0)
             if t >= 0:
+                v_lag(t, 0)
                 v_lag(t, 1)
+            else:
+                fill(6)
             v_vs(t + 3, 1)
             if t >= 0:
                 v_lag(t, 2)
                 v_lag(t, 3)
                 fin1(t - 1)
+            else:
+                fill(8)
             if 0 <= t < 3:
                 prepare_b(t + 5)
             if t >= 0:
@@ -343,23 +348,26 @@ def tile_causalwaveletfieldattentionbyte_pa_kernel(tc, x, k_w, k_b, v_w, v_b, sc
             if 0 <= t < 2:
                 prepare_a(t + 6)
 
-        with tc.manual_schedule(engines={ET.PE, ET.Activation, ET.SP, ET.Pool}):
+        with tc.manual_schedule():
+            fill(0)
             prepare(0)
+            fill(2)
             prepare(1)
+            fill(2)
             prepare(2)
-            for h in range(4):
-                build_t(h)
+            fill(8)
             step(-5)
             prepare(3)
             step(-4)
             step(-3)
-            prepare(4)
+            prepare_a(4)
+            fill(16)
+            prepare_b(4)
             step(-2)
             prepare_a(5)
+            fill(12)
             step(-1)
-            for h in range(4, H):
-                build_t(h)
-        with tc.manual_schedule():
+            fill(8 * H)
             for t in range(NU):
                 step(t)
             fin1(NU - 1)

@@ -51,18 +51,23 @@ def tile_causalwaveletfieldattentionbyte_pa_kernel(tc, x, k_w, k_b, v_w, v_b, sc
         raws = []
         for gi in range(len(groups)):
             view, q, kind = groups[gi]
-            pair = []
-            for half in range(2):
-                raw = ld.tile([P, 2, D], BF16, name="raw%d_%d" % (gi, half))
-                nc.sync.dma_start(out=raw[:], in_=view[:, 4 * q + 2 * half:4 * q + 2 * half + 2, :])
-                pair.append(raw)
-            raws.append(pair)
+            rows = []
+            per = 1 if gi == 0 else 2
+            for part in range(4 // per):
+                raw = ld.tile([P, per, D], BF16, name="raw%d_%d" % (gi, part))
+                nc.sync.dma_start(out=raw[:], in_=view[:, 4 * q + per * part:4 * q + per * (part + 1), :])
+                for j in range(per):
+                    rows.append(raw[:, j, :])
+            raws.append(rows)
 
+        sg_bf = const.tile([P, NS * H], BF16)
+        nc.scalar.dma_start(out=sg_bf[:], in_=scale_gain.rearrange("j h -> (j h)").partition_broadcast(P))
         bias_in = const.tile([P, P], BF16)
         nc.vector.memset(bias_in[:], 0.0)
         nc.scalar.dma_start(out=bias_in[0:CT, :], in_=k_b.rearrange("(c p) -> c p", p=P))
-        sg_bf = const.tile([P, NS * H], BF16)
-        nc.scalar.dma_start(out=sg_bf[:], in_=scale_gain.rearrange("j h -> (j h)").partition_broadcast(P))
+        warm = const.tile([P, 2], F32)
+        nc.vector.memset(warm[:], 1.0)
+        nc.scalar.activation(out=warm[:, 1:2], in_=warm[:, 0:1], func=AF.Exp)
         vbc = const.tile([P, C], BF16)
         nc.scalar.dma_start(out=vbc[:], in_=v_b.partition_broadcast(P))
 
@@ -112,6 +117,7 @@ def tile_causalwaveletfieldattentionbyte_pa_kernel(tc, x, k_w, k_b, v_w, v_b, sc
         nc.vector.tensor_tensor(out=sg[:], in0=sg[:], in1=mx[:].unsqueeze(2).to_broadcast([P, H, NS]), op=ALU.subtract)
         eg = const.tile([P, H, NS], F32)
         nc.scalar.activation(out=eg[:], in_=sg[:], func=AF.Exp)
+        nc.scalar.activation(out=warm[:, 1:2], in_=eg[:, 0, 0:1], func=AF.Sqrt)
         sm = const.tile([P, H], F32)
         nc.vector.tensor_reduce(out=sm[:], in_=eg[:], axis=AX.X, op=ALU.add)
         rs = const.tile([P, H], F32)
@@ -159,7 +165,7 @@ def tile_causalwaveletfieldattentionbyte_pa_kernel(tc, x, k_w, k_b, v_w, v_b, sc
             grouped_of[gi] = grouped
             gw = grouped[:].bitcast(F32)
             for i in range(4):
-                words = raws[gi][i // 2][:, i % 2, :].bitcast(F32)
+                words = raws[gi][i].bitcast(F32)
                 if gi < 6 and i % 2:
                     tp = psv.tile([P, NG, 2, P], F32, tag="v")
                 else:
@@ -278,25 +284,28 @@ def tile_causalwaveletfieldattentionbyte_pa_kernel(tc, x, k_w, k_b, v_w, v_b, sc
                 nc.tensor.transpose(tp[:, i, :], gt_of[u][:, 4 * half + i, :], ident)
             tp_of[(u, half)] = tp
 
-        def v_first(u):
+        def v_first(u, half):
+            if u < 0 or u >= NU:
+                return
             hp = u % CT
             f1v = fsb[u % 3][:, PAD - 1:PAD - 1 + N].rearrange("p (q r) -> p q r", r=R)
-            acc = work.tile([P, N], F32)
-            acc_of[u] = acc
-            accv = acc[:].rearrange("p (q r) -> p q r", r=R)
-            for half in range(2):
-                nc.vector.scalar_tensor_tensor(out=accv[:, :, 4 * half:4 * half + 4], in0=f1v[:, :, 4 * half:4 * half + 4],
-                                               scalar=ca[:, hp, 0:1], in1=tp_of[(u, half)][:].rearrange("p r q -> p q r"),
-                                               op0=ALU.mult, op1=ALU.add)
+            if half == 0:
+                acc = four.tile([P, N], F32, name="acc")
+                acc_of[u] = acc
+            accv = acc_of[u][:].rearrange("p (q r) -> p q r", r=R)
+            nc.vector.scalar_tensor_tensor(out=accv[:, :, 4 * half:4 * half + 4], in0=f1v[:, :, 4 * half:4 * half + 4],
+                                           scalar=ca[:, hp, 0:1], in1=tp_of[(u, half)][:].rearrange("p r q -> p q r"),
+                                           op0=ALU.mult, op1=ALU.add)
 
         short = ((2, ca, 1), (3, cb, 0), (4, ca, 2), (6, cb, 1), (12, cb, 2))
 
-        def v_lag(u, i):
+        def v_lag(u, i, pieces):
             lag, co, j = short[i]
             acc = acc_of[u]
-            for c0 in (0, N // 2):
-                nc.vector.scalar_tensor_tensor(out=acc[:, c0:c0 + N // 2], in0=fsb[u % 3][:, PAD - lag + c0:PAD - lag + c0 + N // 2],
-                                               scalar=co[:, u % CT, j:j + 1], in1=acc[:, c0:c0 + N // 2],
+            w = N // pieces
+            for c0 in range(0, N, w):
+                nc.vector.scalar_tensor_tensor(out=acc[:, c0:c0 + w], in0=fsb[u % 3][:, PAD - lag + c0:PAD - lag + c0 + w],
+                                               scalar=co[:, u % CT, j:j + 1], in1=acc[:, c0:c0 + w],
                                                op0=ALU.mult, op1=ALU.add)
 
         def fin0(u):
@@ -312,10 +321,22 @@ def tile_causalwaveletfieldattentionbyte_pa_kernel(tc, x, k_w, k_b, v_w, v_b, sc
             nc.sync.dma_start(out=out_1[b, hp * P:(hp + 1) * P, :], in_=o8[:].bitcast(U8))
 
 
+        def last_out(u):
+            b, hp = u // CT, u % CT
+            lag, co, j = short[4]
+            acc = acc_of[u]
+            o8 = work.tile([P, N], FP8)
+            for c0 in (0, N // 2):
+                cols = slice(c0, c0 + N // 2)
+                nc.vector.scalar_tensor_tensor(out=acc[:, cols], in0=fsb[u % 3][:, PAD - lag + c0:PAD - lag + c0 + N // 2],
+                                               scalar=co[:, hp, j:j + 1], in1=acc[:, cols], op0=ALU.mult, op1=ALU.add)
+                nc.scalar.activation(out=o8[:, cols], in_=acc[:, cols], func=AF.Copy, scale=Y_SCALE, saturate=False)
+                nc.sync.dma_start(out=out_1[b, hp * P:(hp + 1) * P, cols], in_=o8[:, cols].bitcast(U8))
+                nc.sync.dma_start(out=out_0[b, hp * P:(hp + 1) * P, cols], in_=acc[:, cols])
+
         def step(t):
+            pieces = 1 if t + 3 < NU else 2
             sel_pe(t + 4)
-            if t >= 0:
-                v_first(t)
             v_pe(t + 3, 0)
             k_mx(t + 5, 0)
             v_pe(t + 3, 1)
@@ -327,23 +348,27 @@ def tile_causalwaveletfieldattentionbyte_pa_kernel(tc, x, k_w, k_b, v_w, v_b, sc
             g_mm(t + 2, 0)
             g_mm(t + 2, 1)
             sel_s(t + 4)
+            if t >= 0:
+                v_lag(t, 0, pieces)
             v_vs(t + 3, 0)
             if t >= 0:
-                v_lag(t, 0)
-                v_lag(t, 1)
+                v_lag(t, 1, pieces)
             else:
                 fill(6)
             v_vs(t + 3, 1)
             if t >= 0:
-                v_lag(t, 2)
-                v_lag(t, 3)
-                fin1(t - 1)
+                v_lag(t, 2, pieces)
             else:
                 fill(8)
+            v_first(t + 1, 0)
+            if t >= 0:
+                v_lag(t, 3, pieces)
+                fin1(t - 1)
+            v_first(t + 1, 1)
             if 0 <= t < 3:
                 prepare_b(t + 5)
-            if t >= 0:
-                v_lag(t, 4)
+            if 0 <= t < NU - 1:
+                v_lag(t, 4, pieces)
                 fin0(t)
             if 0 <= t < 2:
                 prepare_a(t + 6)
@@ -370,4 +395,4 @@ def tile_causalwaveletfieldattentionbyte_pa_kernel(tc, x, k_w, k_b, v_w, v_b, sc
             fill(8 * H)
             for t in range(NU):
                 step(t)
-            fin1(NU - 1)
+            last_out(NU - 1)

from contextlib import ExitStack

import concourse.mybir as mybir
from concourse.masks import make_identity

B, N, D, C, H, NS = 2, 1024, 1024, 1024, 16, 10
T0, T1, T2, T3 = 0.4829629131445341, 0.8365163037378079, 0.2241438680420134, -0.1294095225512604
Y_SCALE = 60.0
FLOPS = 2 * 2 * B * N * D * C

F32 = mybir.dt.float32
BF16 = mybir.dt.bfloat16
U32 = mybir.dt.uint32
U8 = mybir.dt.uint8
FP8X4 = mybir.dt.float8_e4m3fn_x4
FP8 = mybir.dt.float8_e4m3fn
AF = mybir.ActivationFunctionType
ALU = mybir.AluOpType
AX = mybir.AxisListType
ET = mybir.EngineType

P = 128
NG = 2
CT = C // P
QW = 512
R = 8
TT = B * R
PAD = 16


def tile_causalwaveletfieldattentionbyte_pa_kernel(tc, x, k_w, k_b, v_w, v_b, scale_gain, out_0, out_1):
    nc = tc.nc
    NT = B * N

    with ExitStack() as ctx:
        const = ctx.enter_context(tc.tile_pool(name="const", bufs=1))
        keep = ctx.enter_context(tc.tile_pool(name="keep", bufs=1))
        ld = ctx.enter_context(tc.tile_pool(name="ld", bufs=1))
        stg = ctx.enter_context(tc.tile_pool(name="stg", bufs=3))
        work = ctx.enter_context(tc.tile_pool(name="work", bufs=3))
        two = ctx.enter_context(tc.tile_pool(name="two", bufs=2))
        four = ctx.enter_context(tc.tile_pool(name="four", bufs=4))
        pss = ctx.enter_context(tc.psum_pool(name="pss", bufs=4))
        psv = ctx.enter_context(tc.psum_pool(name="psv", bufs=4))

        kview = k_w.rearrange("(t p) d -> p t d", p=P)
        vview = v_w.rearrange("(t p) d -> p t d", p=P)
        xviews = [x[b].rearrange("(q r) d -> q r d", r=R) for b in range(B)]
        groups = [(kview, 0, "k"), (xviews[0], 0, "x0"), (xviews[0], 1, "x0"), (vview, 0, "v"),
                  (kview, 1, "k"), (vview, 1, "v"), (xviews[1], 0, "x1"), (xviews[1], 1, "x1")]
        raws = []
        for gi in range(len(groups)):
            view, q, kind = groups[gi]
            rows = []
            per = 1 if gi == 0 else 2
            for part in range(4 // per):
                raw = ld.tile([P, per, D], BF16, name="raw%d_%d" % (gi, part))
                nc.sync.dma_start(out=raw[:], in_=view[:, 4 * q + per * part:4 * q + per * (part + 1), :])
                for j in range(per):
                    rows.append(raw[:, j, :])
            raws.append(rows)

        sg_bf = const.tile([P, NS * H], BF16)
        nc.scalar.dma_start(out=sg_bf[:], in_=scale_gain.rearrange("j h -> (j h)").partition_broadcast(P))
        bias_in = const.tile([P, P], BF16)
        nc.vector.memset(bias_in[:], 0.0)
        nc.scalar.dma_start(out=bias_in[0:CT, :], in_=k_b.rearrange("(c p) -> c p", p=P))
        warm = const.tile([P, 2], F32)
        nc.vector.memset(warm[:], 1.0)
        nc.scalar.activation(out=warm[:, 1:2], in_=warm[:, 0:1], func=AF.Exp)
        vbc = const.tile([P, C], BF16)
        nc.scalar.dma_start(out=vbc[:], in_=v_b.partition_broadcast(P))

        ipad = const.tile([P, 2 * P], F32)
        nc.gpsimd.memset(ipad[:], 0.0)
        make_identity(nc, ipad[:, P:2 * P])
        ident = ipad[:, P:2 * P]

        def shifted(dq):
            return ipad[:, P - dq:2 * P - dq]

        ident_bf = const.tile([P, P], BF16)
        make_identity(nc, ident_bf[:])
        tiny = const.tile([P, 1], F32)
        nc.vector.memset(tiny[:], 1e-30)
        sel2 = const.tile([P, 2], F32)
        nc.vector.memset(sel2[:], 0.0)
        nc.vector.memset(sel2[0:64, 0:1], 1.0)
        nc.vector.memset(sel2[64:128, 1:2], 1.0)
        fsb = []
        for i in range(3):
            t = const.tile([P, PAD + N], F32, name="fsb%d" % i)
            nc.vector.memset(t[:, 0:PAD], 0.0)
            fsb.append(t)

        yc = const.tile([P, R, P], F32)
        nc.vector.tensor_scalar(out=yc[:, 0, :], in0=shifted(1), scalar1=T1, scalar2=None, op0=ALU.mult)
        for i in range(1, 8):
            dq = 2 ** (i - 1)
            nc.vector.tensor_scalar(out=yc[:, i, :], in0=shifted(dq), scalar1=T2, scalar2=None, op0=ALU.mult)
            for mul, tap in ((2, T1), (3, T0)):
                if mul * dq < P:
                    nc.vector.scalar_tensor_tensor(out=yc[:, i, :], in0=shifted(mul * dq), scalar=tap, in1=yc[:, i, :],
                                                   op0=ALU.mult, op1=ALU.add)
        t3i = const.tile([P, P], F32)
        nc.vector.tensor_scalar(out=t3i[:], in0=ident, scalar1=T3, scalar2=None, op0=ALU.mult)

        bps = psv.tile([P, P], BF16, tag="v")
        nc.tensor.transpose(bps[:], bias_in[:], ident_bf[:])
        kbias = const.tile([P, CT], F32)
        nc.vector.tensor_copy(out=kbias[:], in_=bps[:, 0:CT])

        sg = const.tile([P, H, NS], F32)
        nc.vector.tensor_copy(out=sg[:], in_=sg_bf[:].rearrange("p (j h) -> p h j", h=H))
        mx = const.tile([P, H], F32)
        nc.vector.tensor_reduce(out=mx[:], in_=sg[:], axis=AX.X, op=ALU.max)
        nc.vector.tensor_tensor(out=sg[:], in0=sg[:], in1=mx[:].unsqueeze(2).to_broadcast([P, H, NS]), op=ALU.subtract)
        eg = const.tile([P, H, NS], F32)
        nc.scalar.activation(out=eg[:], in_=sg[:], func=AF.Exp)
        nc.scalar.activation(out=warm[:, 1:2], in_=eg[:, 0, 0:1], func=AF.Sqrt)
        sm = const.tile([P, H], F32)
        nc.vector.tensor_reduce(out=sm[:], in_=eg[:], axis=AX.X, op=ALU.add)
        rs = const.tile([P, H], F32)
        nc.vector.reciprocal(out=rs[:], in_=sm[:])
        nc.vector.tensor_tensor(out=eg[:], in0=eg[:], in1=rs[:].unsqueeze(2).to_broadcast([P, H, NS]), op=ALU.mult)
        gsel = const.tile([P, CT, NS], F32)
        for s in range(2):
            rows = slice(64 * s, 64 * s + 64)
            nc.vector.tensor_copy(out=gsel[rows], in_=eg[rows].rearrange("p (c s) j -> p s c j", s=2)[:, s])
        ca = const.tile([P, CT, NS], F32)
        nc.vector.tensor_scalar(out=ca[:], in0=gsel[:], scalar1=T2, scalar2=None, op0=ALU.mult)
        nc.vector.scalar_tensor_tensor(out=ca[:, :, 1:NS], in0=gsel[:, :, 0:NS - 1], scalar=T1, in1=ca[:, :, 1:NS],
                                       op0=ALU.mult, op1=ALU.add)
        cb = const.tile([P, CT, NS], F32)
        nc.vector.tensor_scalar(out=cb[:], in0=gsel[:], scalar1=T0, scalar2=None, op0=ALU.mult)

        th = const.tile([P, H, P], F32)

        built = [0]

        def fill(n):
            for c in range(built[0], min(built[0] + n, 8 * H)):
                h, i = 4 * (c // 32) + c % 4, (c % 32) // 4
                if i == 0:
                    nc.vector.scalar_tensor_tensor(out=th[:, h, :], in0=yc[:, 0, :], scalar=eg[:, h, 2:3], in1=t3i[:],
                                                   op0=ALU.mult, op1=ALU.add)
                else:
                    dq = 2 ** (i - 1)
                    nc.vector.scalar_tensor_tensor(out=th[:, h, dq:P], in0=yc[:, i, dq:P], scalar=eg[:, h, i + 2:i + 3],
                                                   in1=th[:, h, dq:P], op0=ALU.mult, op1=ALU.add)
            built[0] = min(built[0] + n, 8 * H)

        xc = keep.tile([P, NG, NT], U32, align_bytes=64)
        xs = keep.tile([P, NG, NT], U8, align_bytes=64)
        kc = keep.tile([P, NG, C], U32, align_bytes=64)
        ks = keep.tile([P, NG, C], U8, align_bytes=64)
        vc = keep.tile([P, NG, C], U32, align_bytes=64)
        vs = keep.tile([P, NG, C], U8, align_bytes=64)
        dest = {"k": (kc, ks, 0), "v": (vc, vs, 0), "x0": (xc, xs, 0), "x1": (xc, xs, N)}

        grouped_of = {}

        def prepare_a(gi):
            grouped = stg.tile([P, NG, 4 * QW], BF16, align_bytes=64)
            grouped_of[gi] = grouped
            gw = grouped[:].bitcast(F32)
            for i in range(4):
                words = raws[gi][i].bitcast(F32)
                if gi < 6 and i % 2:
                    tp = psv.tile([P, NG, 2, P], F32, tag="v")
                else:
                    tp = pss.tile([P, NG, 2, P], F32, tag="s")
                for g in range(NG):
                    for u in range(2):
                        nc.tensor.transpose(tp[:, g, u, :], words[:, 256 * g + u:256 * (g + 1):2], ident)
                dst = gw[:, :, 2 * P * i:2 * P * (i + 1)].rearrange("p g (r u) -> p g r u", u=2)
                nc.scalar.copy(out=dst, in_=tp[:].rearrange("p g u r -> p g r u"))

        def prepare_b(gi):
            view, q, kind = groups[gi]
            codes, scales, base = dest[kind]
            cols = slice(base + q * QW, base + (q + 1) * QW)
            for g in range(NG):
                nc.vector.quantize_mx(out=codes[:, g, cols].bitcast(FP8X4), scales=scales[:, g, cols],
                                      in_=grouped_of[gi][:, g, :])

        def prepare(gi):
            prepare_a(gi)
            prepare_b(gi)

        NU = B * CT
        k2_of, mt_of, ft_of, gt_of, tp_of, acc_of, m2_of, vps_of, m2c_of = {}, {}, {}, {}, {}, {}, {}, {}, {}

        def k_mx(u, c):
            if u < 0 or u >= NU:
                return
            b, hp = u // CT, u % CT
            ch = slice(hp * P, (hp + 1) * P)
            if c == 0:
                k2 = work.tile([P, N], F32, name="k2")
                k2_of[u] = k2
            tok = slice(b * N + c * 512, b * N + (c + 1) * 512)
            kps = pss.tile([P, 512], F32, tag="s")
            for g in range(NG):
                nc.tensor.matmul_mx(out=kps[:], lhsT=kc[:, g, ch].bitcast(FP8X4), lhsT_scale=ks[:, g, ch],
                                    rhs=xc[:, g, tok].bitcast(FP8X4), rhs_scale=xs[:, g, tok],
                                    start=(g == 0), stop=(g == NG - 1))
            nc.scalar.activation(out=k2_of[u][:, c * 512:(c + 1) * 512], in_=kps[:], func=AF.Square,
                                 bias=kbias[:, hp:hp + 1], scale=1.0)

        def sel_pe(u):
            if u < 0 or u >= NU:
                return
            m2 = psv.tile([P, R, 2], F32, tag="v")
            m2_of[u] = m2
            for r in range(R):
                nc.tensor.matmul(out=m2[:, r, :], lhsT=k2_of[u][:, r * P:(r + 1) * P], rhs=sel2[:], start=True, stop=True)

        def sel_s(u):
            if u < 0 or u >= NU:
                return
            mt = four.tile([P, R, 2], F32, name="mt")
            nc.scalar.activation(out=mt[:], in_=m2_of[u][:], func=AF.Sqrt, bias=tiny[:, 0:1], scale=1.0)
            mt_of[u] = mt

        def v_pe(u, c):
            if u < 0 or u >= NU:
                return
            b, hp = u // CT, u % CT
            ch = slice(hp * P, (hp + 1) * P)
            vps = psv.tile([P, 4, P], F32, tag="v")
            vps_of[(u, c)] = vps
            for i in range(4):
                t0 = b * N + (4 * c + i) * P
                tok = slice(t0, t0 + P)
                for g in range(NG):
                    nc.tensor.matmul_mx(out=vps[:, i, :], lhsT=xc[:, g, tok].bitcast(FP8X4), lhsT_scale=xs[:, g, tok],
                                        rhs=vc[:, g, ch].bitcast(FP8X4), rhs_scale=vs[:, g, ch],
                                        start=(g == 0), stop=(g == NG - 1))

        def v_vs(u, c):
            if u < 0 or u >= NU:
                return
            hp = u % CT
            ch = slice(hp * P, (hp + 1) * P)
            if c == 0:
                ft = four.tile([P, R, P], F32, name="ft")
                ft_of[u] = ft
            vb = work.tile([P, 4, P], F32)
            nc.vector.tensor_tensor(out=vb[:], in0=vps_of[(u, c)][:], in1=vbc[:, ch].unsqueeze(1).to_broadcast([P, 4, P]),
                                    op=ALU.add)
            for i in range(4):
                r = 4 * c + i
                for s in range(2):
                    nc.scalar.activation(out=ft_of[u][:, r, 64 * s:64 * s + 64], in_=vb[:, i, 64 * s:64 * s + 64],
                                         func=AF.Copy, scale=mt_of[u][:, r, s:s + 1])

        def g_mm(u, s):
            if u < 0 or u >= NU:
                return
            hp = u % CT
            if s == 0:
                gt = work.tile([P, R, P], F32, name="gt")
                gt_of[u] = gt
            gps = pss.tile([P, R, 64], F32, tag="s")
            nc.tensor.matmul(out=gps[:], lhsT=th[:, 2 * hp + s, :], rhs=ft_of[u][:, :, 64 * s:64 * s + 64],
                             start=True, stop=True)
            nc.scalar.copy(out=gt_of[u][:, :, 64 * s:64 * s + 64], in_=gps[:])

        def c_f(u, half):
            if u < 0 or u >= NU:
                return
            fsv = fsb[u % 3][:, PAD:PAD + N].rearrange("p (q r) -> p q r", r=R)
            fp = pss.tile([P, 4, P], F32, tag="s")
            for i in range(4):
                nc.tensor.transpose(fp[:, i, :], ft_of[u][:, 4 * half + i, :], ident)
            nc.scalar.copy(out=fsv[:, :, 4 * half:4 * half + 4], in_=fp[:].rearrange("p r q -> p q r"))

        def c_g(u, half):
            if u < 0 or u >= NU:
                return
            tp = psv.tile([P, 4, P], F32, tag="v")
            for i in range(4):
                nc.tensor.transpose(tp[:, i, :], gt_of[u][:, 4 * half + i, :], ident)
            tp_of[(u, half)] = tp

        def v_first(u, half):
            if u < 0 or u >= NU:
                return
            hp = u % CT
            f1v = fsb[u % 3][:, PAD - 1:PAD - 1 + N].rearrange("p (q r) -> p q r", r=R)
            if half == 0:
                acc = four.tile([P, N], F32, name="acc")
                acc_of[u] = acc
            accv = acc_of[u][:].rearrange("p (q r) -> p q r", r=R)
            nc.vector.scalar_tensor_tensor(out=accv[:, :, 4 * half:4 * half + 4], in0=f1v[:, :, 4 * half:4 * half + 4],
                                           scalar=ca[:, hp, 0:1], in1=tp_of[(u, half)][:].rearrange("p r q -> p q r"),
                                           op0=ALU.mult, op1=ALU.add)

        short = ((2, ca, 1), (3, cb, 0), (4, ca, 2), (6, cb, 1), (12, cb, 2))

        def v_lag(u, i, pieces):
            lag, co, j = short[i]
            acc = acc_of[u]
            w = N // pieces
            for c0 in range(0, N, w):
                nc.vector.scalar_tensor_tensor(out=acc[:, c0:c0 + w], in0=fsb[u % 3][:, PAD - lag + c0:PAD - lag + c0 + w],
                                               scalar=co[:, u % CT, j:j + 1], in1=acc[:, c0:c0 + w],
                                               op0=ALU.mult, op1=ALU.add)

        def fin0(u):
            b, hp = u // CT, u % CT
            nc.sync.dma_start(out=out_0[b, hp * P:(hp + 1) * P, :], in_=acc_of[u][:])

        def fin1(u):
            if u < 0:
                return
            b, hp = u // CT, u % CT
            o8 = work.tile([P, N], FP8)
            nc.scalar.activation(out=o8[:], in_=acc_of[u][:], func=AF.Copy, scale=Y_SCALE, saturate=False)
            nc.sync.dma_start(out=out_1[b, hp * P:(hp + 1) * P, :], in_=o8[:].bitcast(U8))


        def last_out(u):
            b, hp = u // CT, u % CT
            lag, co, j = short[4]
            acc = acc_of[u]
            o8 = work.tile([P, N], FP8)
            for c0 in (0, N // 2):
                cols = slice(c0, c0 + N // 2)
                nc.vector.scalar_tensor_tensor(out=acc[:, cols], in0=fsb[u % 3][:, PAD - lag + c0:PAD - lag + c0 + N // 2],
                                               scalar=co[:, hp, j:j + 1], in1=acc[:, cols], op0=ALU.mult, op1=ALU.add)
                nc.scalar.activation(out=o8[:, cols], in_=acc[:, cols], func=AF.Copy, scale=Y_SCALE, saturate=False)
                nc.sync.dma_start(out=out_1[b, hp * P:(hp + 1) * P, cols], in_=o8[:, cols].bitcast(U8))
                nc.sync.dma_start(out=out_0[b, hp * P:(hp + 1) * P, cols], in_=acc[:, cols])

        def step(t):
            pieces = 1 if t + 3 < NU else 2
            sel_pe(t + 4)
            v_pe(t + 3, 0)
            k_mx(t + 5, 0)
            v_pe(t + 3, 1)
            k_mx(t + 5, 1)
            c_f(t + 1, 0)
            c_g(t + 1, 0)
            c_f(t + 1, 1)
            c_g(t + 1, 1)
            g_mm(t + 2, 0)
            g_mm(t + 2, 1)
            sel_s(t + 4)
            if t >= 0:
                v_lag(t, 0, pieces)
            v_vs(t + 3, 0)
            if t >= 0:
                v_lag(t, 1, pieces)
            else:
                fill(6)
            v_vs(t + 3, 1)
            if t >= 0:
                v_lag(t, 2, pieces)
            else:
                fill(8)
            v_first(t + 1, 0)
            if t >= 0:
                v_lag(t, 3, pieces)
                fin1(t - 1)
            v_first(t + 1, 1)
            if 0 <= t < 3:
                prepare_b(t + 5)
            if 0 <= t < NU - 1:
                v_lag(t, 4, pieces)
                fin0(t)
            if 0 <= t < 2:
                prepare_a(t + 6)

        with tc.manual_schedule():
            fill(0)
            prepare(0)
            fill(2)
            prepare(1)
            fill(2)
            prepare(2)
            fill(8)
            step(-5)
            prepare(3)
            step(-4)
            step(-3)
            prepare_a(4)
            fill(16)
            prepare_b(4)
            step(-2)
            prepare_a(5)
            fill(12)
            step(-1)
            fill(8 * H)
            for t in range(NU):
                step(t)
            last_out(NU - 1)
